import numpy as np
import ml_dtypes


def mxq(x, axis, fmt="e4m3"):
    dtype, down = {"e4m3": (ml_dtypes.float8_e4m3fn, 7), "e5m2": (ml_dtypes.float8_e5m2, 14)}[fmt]
    v = np.moveaxis(np.asarray(x, np.float32).astype(ml_dtypes.bfloat16).astype(np.float64), axis, -1)
    blocks = v.reshape(v.shape[:-1] + (-1, 32))
    amax = np.abs(blocks).max(-1, keepdims=True)
    byte = np.maximum(np.where(amax > 0, np.frexp(amax)[1] - 1 + 127, 0) - down, 1)
    scale = np.exp2(byte - 127.0)
    codes = (blocks / scale).astype(np.float32).astype(dtype).astype(np.float64)
    return np.moveaxis((codes * scale).reshape(v.shape), -1, axis)


WIDE = False


def mx_kscale(k):
    if not WIDE:
        return np.ones(k)
    levels = np.array([10, -10, 5, -5, 0])
    a = np.random.permutation(np.resize(levels, k // 512 * 4)).reshape(k // 512, 4)
    idx = np.arange(k)
    return np.exp2(a[idx // 512, idx % 128 // 32])


BF16 = ml_dtypes.bfloat16


def bf(x):
    return np.asarray(x, np.float32).astype(BF16)


def f64(x):
    return np.asarray(x).astype(np.float64)


B, N, HID, ITERS = 512, 32, 2048, 10
DIN = 2 * N * N
SLOPE = 0.01


def leaky(v):
    return np.where(v >= 0.0, v, SLOPE * v)


def setup_inputs():
    s, t = mx_kscale(DIN), mx_kscale(HID)
    sp, sq = s[0::2].reshape(N, N), s[1::2].reshape(N, N)
    return {"p": bf(np.random.uniform(size=(B, N, N)) * sp),
            "q": bf(np.random.uniform(size=(B, N, N)) * sq),
            "W1": bf(np.random.standard_normal((DIN, HID)) * 1.7 / np.sqrt(DIN) / s[:, None] * t),
            "b1": bf(np.random.standard_normal(HID) * 0.3 * t),
            "W2": bf(np.random.standard_normal((HID, HID)) * 1.4 / np.sqrt(HID) / t[:, None]),
            "b2": bf(np.random.standard_normal(HID) * 0.3)}


def reference(p, q, W1, b1, W2, b2):
    x = np.stack([f64(p), f64(q)], axis=-1).reshape(B, DIN)
    h1 = leaky((mxq(x, 1, "e4m3") @ mxq(f64(W1), 0, "e4m3")) + f64(b1))
    return leaky((mxq(h1, 1, "e4m3") @ mxq(f64(W2), 0, "e4m3")) + f64(b2))

@@ -1,0 +1,276 @@
+from contextlib import ExitStack
+
+import concourse.mybir as mybir
+from concourse.masks import make_identity
+
+F32 = mybir.dt.float32
+BF16 = mybir.dt.bfloat16
+U32 = mybir.dt.uint32
+U8 = mybir.dt.uint8
+FP8X4 = mybir.dt.float8_e4m3fn_x4
+ALU = mybir.AluOpType
+ACT = mybir.ActivationFunctionType
+
+P = 128
+PACK = 4
+K_PASS = P * PACK
+BATCH = 512
+WIDTH = 2048
+SLOPE = 0.01
+PASSES = WIDTH // K_PASS
+SAMPLE_TILES = BATCH // P
+
+BLOCK_COLS = 512
+BLOCKS = WIDTH // BLOCK_COLS
+BLOCK_BANKS = 4
+CHUNK_PASSES = 2
+CHUNK_ROWS = CHUNK_PASSES * K_PASS
+BLOCK_CHUNKS = PASSES // CHUNK_PASSES
+LAYER_CHUNKS = BLOCKS * BLOCK_CHUNKS
+CHUNKS = 2 * LAYER_CHUNKS
+
+RAW_BUFS = 10
+RUN = 4
+
+VECTOR_COLS = 256
+VECTOR_CHUNKS = 12
+
+QUANTISE_LAG = 1
+MULTIPLY_LAG = 2
+BIAS_LAG = 2
+LEAKY_LAG = 3
+REQUANTISE_LAG = 4
+FINISH_LAG = 2
+
+FLOPS = 2 * 2 * BATCH * WIDTH * WIDTH
+
+
+def tile_matchingnet_pb_kernel(tc, p, q, W1, b1, W2, b2, out):
+    nc = tc.nc
+    with ExitStack() as ctx:
+        keep = ctx.enter_context(tc.tile_pool(name="keep", bufs=1))
+        raw_pool = ctx.enter_context(tc.tile_pool(name="raw", bufs=RAW_BUFS))
+        grouped_pool = ctx.enter_context(tc.tile_pool(name="grouped", bufs=4))
+        weight_pool = ctx.enter_context(tc.tile_pool(name="weight", bufs=4))
+        hidden_pool = ctx.enter_context(tc.tile_pool(name="hidden", bufs=2))
+        result_pool = ctx.enter_context(tc.tile_pool(name="result", bufs=3))
+        psum = ctx.enter_context(tc.psum_pool(name="psum", bufs=8))
+
+        raw_of = {}
+        grouped_of = {}
+        codes_of = {}
+        scales_of = {}
+        banks_of = {}
+        biased_of = {}
+        hidden_of = {}
+
+        x_codes = keep.tile([P, PASSES, BATCH], U32, align_bytes=64)
+        x_scales = keep.tile([P, PASSES, BATCH], U8, align_bytes=64)
+        h_codes = keep.tile([P, PASSES, BATCH], U32, align_bytes=64)
+        h_scales = keep.tile([P, PASSES, BATCH], U8, align_bytes=64)
+        p_rows = keep.tile([P, SAMPLE_TILES * WIDTH // 2], BF16)
+        q_rows = keep.tile([P, SAMPLE_TILES * WIDTH // 2], BF16)
+        b1_rows = keep.tile([P, P], BF16)
+        b1_cols = keep.tile([P, WIDTH // P], F32)
+        b2_all = keep.tile([P, WIDTH], BF16)
+        ident_f32 = keep.tile([P, P], F32)
+        ident_bf16 = keep.tile([P, P], BF16)
+
+        def place(chunk):
+            layer, rest = divmod(chunk, LAYER_CHUNKS)
+            block, half = divmod(rest, BLOCK_CHUNKS)
+            return layer, block, half
+
+        def load_weights(chunk):
+            layer, block, half = place(chunk)
+            rows = slice(half * CHUNK_ROWS, (half + 1) * CHUNK_ROWS)
+            cols = slice(block * BLOCK_COLS, (block + 1) * BLOCK_COLS)
+            raw = raw_pool.tile([P, CHUNK_PASSES, PACK, BLOCK_COLS], BF16)
+            if layer == 0:
+                by_place = W1[rows, cols].rearrange(
+                    "(c r u e) w -> e u r c w", c=CHUNK_PASSES, u=2, e=2
+                )
+                for e in range(2):
+                    for u in range(2):
+                        nc.sync.dma_start(out=raw[:, :, 2 * e + u, :], in_=by_place[e, u])
+            else:
+                nc.sync.dma_start(
+                    out=raw[:].rearrange("r c t w -> r (c t) w"),
+                    in_=W2[rows, cols].rearrange("(ct r) w -> r ct w", r=P),
+                )
+            raw_of[chunk] = raw
+
+        def regroup(chunk):
+            split = (VECTOR_COLS if chunk < VECTOR_CHUNKS else 0) // RUN
+            raw = raw_of[chunk]
+            grouped = grouped_pool.tile([P, CHUNK_PASSES, BLOCK_COLS, PACK], BF16, align_bytes=64)
+            for c in range(CHUNK_PASSES):
+                src = raw[:, c, :, :].rearrange("r t (w i) -> r w t i", i=RUN)
+                dst = grouped[:, c, :, :].rearrange("r (w i) t -> r w t i", i=RUN)
+                if split > 0:
+                    nc.vector.tensor_copy(out=dst[:, :split, :, :], in_=src[:, :split, :, :])
+                nc.scalar.copy(out=dst[:, split:, :, :], in_=src[:, split:, :, :])
+            grouped_of[chunk] = grouped
+
+        def quantise_weights(chunk):
+            codes = weight_pool.tile([P, CHUNK_PASSES * BLOCK_COLS], U32, align_bytes=64)
+            scales = weight_pool.tile([P, CHUNK_PASSES * BLOCK_COLS], U8, align_bytes=64)
+            nc.vector.quantize_mx(
+                out=codes[:].bitcast(FP8X4),
+                scales=scales[:],
+                in_=grouped_of[chunk][:].rearrange("r c w t -> r (c w t)"),
+            )
+            codes_of[chunk] = codes
+            scales_of[chunk] = scales
+
+        def multiply(chunk):
+            layer, block, half = place(chunk)
+            if half == 0:
+                banks_of[layer, block] = [
+                    psum.tile([P, BLOCK_COLS], F32, tag="bank", name="acc%d" % b)
+                    for b in range(BLOCK_BANKS)
+                ]
+            codes = codes_of[chunk]
+            scales = scales_of[chunk]
+            for b in range(BLOCK_BANKS):
+                tile_cols = slice(b * P, (b + 1) * P)
+                for c in range(CHUNK_PASSES):
+                    k_pass = half * CHUNK_PASSES + c
+                    first = c * BLOCK_COLS
+                    if layer == 0:
+                        units = slice(first + b * P, first + (b + 1) * P)
+                        lhsT, lhsT_scale = codes[:, units], scales[:, units]
+                        rhs, rhs_scale = x_codes[:, k_pass, :], x_scales[:, k_pass, :]
+                    else:
+                        lhsT, lhsT_scale = h_codes[:, k_pass, tile_cols], h_scales[:, k_pass, tile_cols]
+                        columns = slice(first, first + BLOCK_COLS)
+                        rhs, rhs_scale = codes[:, columns], scales[:, columns]
+                    nc.tensor.matmul_mx(
+                        out=banks_of[layer, block][b][:],
+                        lhsT=lhsT.bitcast(FP8X4),
+                        lhsT_scale=lhsT_scale,
+                        rhs=rhs.bitcast(FP8X4),
+                        rhs_scale=rhs_scale,
+                        start=(k_pass == 0),
+                        stop=(k_pass == PASSES - 1),
+                    )
+
+        def prepare_inputs():
+            b1_bank = psum.tile([P, P], BF16, tag="bank")
+            nc.tensor.transpose(b1_bank[:], b1_rows[:], ident_bf16[:])
+            nc.vector.tensor_copy(out=b1_cols[:], in_=b1_bank[:, : WIDTH // P])
+
+            words_of_table = (p_rows[:].bitcast(F32), q_rows[:].bitcast(F32))
+            sample_words = WIDTH // 4
+            grouped_x = {}
+            for k_pass in range(PASSES + 1):
+                if k_pass < PASSES:
+                    x_tile = hidden_pool.tile([P, BATCH * PACK], BF16, tag="x", align_bytes=64)
+                    x_words = x_tile[:].bitcast(F32).rearrange("r (n e) -> r n e", e=2)
+                    for pair in range(SAMPLE_TILES // 2):
+                        bank = psum.tile([P, 2, 2 * P], F32, tag="bank")
+                        for e in range(2):
+                            for s in range(2):
+                                first = (2 * pair + s) * sample_words + k_pass * P
+                                nc.tensor.transpose(
+                                    bank[:, e, s * P : (s + 1) * P],
+                                    words_of_table[e][:, first : first + P],
+                                    ident_f32[:],
+                                )
+                        copy = nc.scalar.copy if pair % 2 == 0 else nc.vector.tensor_copy
+                        copy(
+                            out=x_words[:, pair * 2 * P : (pair + 1) * 2 * P, :],
+                            in_=bank[:].rearrange("r e n -> r n e"),
+                        )
+                    grouped_x[k_pass] = x_tile
+                if k_pass > 0:
+                    nc.vector.quantize_mx(
+                        out=x_codes[:, k_pass - 1, :].bitcast(FP8X4),
+                        scales=x_scales[:, k_pass - 1, :],
+                        in_=grouped_x[k_pass - 1][:],
+                    )
+
+        def add_hidden_bias(block):
+            biased = hidden_pool.tile([P, PACK, BATCH], F32)
+            for t in range(PACK):
+                unit_tile = block * PACK + t
+                nc.scalar.activation(
+                    out=biased[:, t, :],
+                    in_=banks_of[0, block][t][:],
+                    func=ACT.Identity,
+                    bias=b1_cols[:, unit_tile : unit_tile + 1],
+                    scale=1.0,
+                )
+            biased_of[block] = biased
+
+        def leaky_hidden(block):
+            hidden = hidden_pool.tile([P, BATCH, PACK], BF16, align_bytes=64)
+            by_sample = biased_of[block][:].rearrange("r t n -> r n t")
+            nc.vector.scalar_tensor_tensor(
+                out=hidden[:], in0=by_sample, scalar=SLOPE, in1=by_sample, op0=ALU.mult, op1=ALU.max
+            )
+            hidden_of[block] = hidden
+
+        def quantise_hidden(block):
+            nc.vector.quantize_mx(
+                out=h_codes[:, block, :].bitcast(FP8X4),
+                scales=h_scales[:, block, :],
+                in_=hidden_of[block][:].rearrange("r n t -> r (n t)"),
+            )
+
+        def finish_output(block, first_tile):
+            cols = slice(block * BLOCK_COLS, (block + 1) * BLOCK_COLS)
+            biased = result_pool.tile([P, 2, BLOCK_COLS], F32, tag="biased_out")
+            for s in range(2):
+                nc.vector.tensor_tensor(
+                    out=biased[:, s, :],
+                    in0=banks_of[1, block][first_tile + s][:],
+                    in1=b2_all[:, cols],
+                    op=ALU.add,
+                )
+            result = result_pool.tile([P, 2, BLOCK_COLS], F32)
+            nc.vector.scalar_tensor_tensor(
+                out=result[:], in0=biased[:], scalar=SLOPE, in1=biased[:], op0=ALU.mult, op1=ALU.max
+            )
+            rows = out.rearrange("(r s) j -> r s j", s=SAMPLE_TILES)
+            nc.sync.dma_start(out=rows[:, first_tile : first_tile + 2, cols], in_=result[:])
+
+        make_identity(nc, ident_f32[:])
+        make_identity(nc, ident_bf16[:])
+        nc.vector.memset(b1_rows[:], 0.0)
+        nc.scalar.dma_start(out=b1_rows[: WIDTH // P, :], in_=b1.rearrange("(t r) -> t r", r=P))
+        load_weights(0)
+        nc.sync.dma_start(out=p_rows[:], in_=p.rearrange("(r s) i j -> r (s i j)", s=SAMPLE_TILES))
+        nc.sync.dma_start(out=q_rows[:], in_=q.rearrange("(r s) i j -> r (s i j)", s=SAMPLE_TILES))
+        for chunk in range(1, RAW_BUFS):
+            load_weights(chunk)
+        nc.sync.dma_start(out=b2_all[:], in_=b2.partition_broadcast(P))
+
+        def completed(step, lag, layer):
+            chunk = step - lag
+            if 0 <= chunk < CHUNKS and chunk % BLOCK_CHUNKS == BLOCK_CHUNKS - 1:
+                if place(chunk)[0] == layer:
+                    return place(chunk)[1]
+            return None
+
+        for step in range(CHUNKS + FINISH_LAG + 2):
+            if step < CHUNKS:
+                regroup(step)
+            if step + RAW_BUFS < CHUNKS:
+                load_weights(step + RAW_BUFS)
+            if step == 0:
+                prepare_inputs()
+            if completed(step, REQUANTISE_LAG, 0) is not None:
+                quantise_hidden(completed(step, REQUANTISE_LAG, 0))
+            if 0 <= step - QUANTISE_LAG < CHUNKS:
+                quantise_weights(step - QUANTISE_LAG)
+            if 0 <= step - MULTIPLY_LAG < CHUNKS:
+                multiply(step - MULTIPLY_LAG)
+            if completed(step, BIAS_LAG, 0) is not None:
+                add_hidden_bias(completed(step, BIAS_LAG, 0))
+            if completed(step, LEAKY_LAG, 0) is not None:
+                leaky_hidden(completed(step, LEAKY_LAG, 0))
+            if completed(step, FINISH_LAG, 1) is not None:
+                finish_output(completed(step, FINISH_LAG, 1), 0)
+            if completed(step, FINISH_LAG + 1, 1) is not None:
+                finish_output(completed(step, FINISH_LAG + 1, 1), 2)

@@ -87,17 +87,16 @@ def tile_matchingnet_pb_kernel(tc, p, q, W1, b1, W2, b2, out):
             cols = slice(block * BLOCK_COLS, (block + 1) * BLOCK_COLS)
             raw = raw_pool.tile([P, CHUNK_PASSES, PACK, BLOCK_COLS], BF16)
             if layer == 0:
-                by_place = W1[rows, cols].rearrange(
-                    "(c r u e) w -> e u r c w", c=CHUNK_PASSES, u=2, e=2
+                by_table = W1[rows, cols].rearrange(
+                    "(c r u e) w -> c e r u w", c=CHUNK_PASSES, u=2, e=2
                 )
-                for e in range(2):
-                    for u in range(2):
-                        nc.sync.dma_start(out=raw[:, :, 2 * e + u, :], in_=by_place[e, u])
+                for c in range(CHUNK_PASSES):
+                    for e in range(2):
+                        nc.sync.dma_start(out=raw[:, c, 2 * e : 2 * e + 2, :], in_=by_table[c, e])
             else:
-                nc.sync.dma_start(
-                    out=raw[:].rearrange("r c t w -> r (c t) w"),
-                    in_=W2[rows, cols].rearrange("(ct r) w -> r ct w", r=P),
-                )
+                by_pass = W2[rows, cols].rearrange("(c t r) w -> c r t w", c=CHUNK_PASSES, r=P)
+                for c in range(CHUNK_PASSES):
+                    nc.sync.dma_start(out=raw[:, c, :, :], in_=by_pass[c])
             raw_of[chunk] = raw
 
         def regroup(chunk):

@@ -33,7 +33,7 @@ RAW_BUFS = 10
 RUN = 4
 
 VECTOR_COLS = 256
-VECTOR_CHUNKS = 12
+VECTOR_CHUNKS = 11
 
 QUANTISE_LAG = 1
 MULTIPLY_LAG = 2
@@ -63,6 +63,7 @@ def tile_matchingnet_pb_kernel(tc, p, q, W1, b1, W2, b2, out):
         banks_of = {}
         biased_of = {}
         hidden_of = {}
+        biased_out_of = {}
 
         x_codes = keep.tile([P, PASSES, BATCH], U32, align_bytes=64)
         x_scales = keep.tile([P, PASSES, BATCH], U8, align_bytes=64)
@@ -103,12 +104,12 @@ def tile_matchingnet_pb_kernel(tc, p, q, W1, b1, W2, b2, out):
             split = (VECTOR_COLS if chunk < VECTOR_CHUNKS else 0) // RUN
             raw = raw_of[chunk]
             grouped = grouped_pool.tile([P, CHUNK_PASSES, BLOCK_COLS, PACK], BF16, align_bytes=64)
+            src = raw[:].rearrange("r c t (w i) -> r c w t i", i=RUN)
+            dst = grouped[:].rearrange("r c (w i) t -> r c w t i", i=RUN)
+            if split > 0:
+                nc.vector.tensor_copy(out=dst[:, :, :split, :, :], in_=src[:, :, :split, :, :])
             for c in range(CHUNK_PASSES):
-                src = raw[:, c, :, :].rearrange("r t (w i) -> r w t i", i=RUN)
-                dst = grouped[:, c, :, :].rearrange("r (w i) t -> r w t i", i=RUN)
-                if split > 0:
-                    nc.vector.tensor_copy(out=dst[:, :split, :, :], in_=src[:, :split, :, :])
-                nc.scalar.copy(out=dst[:, split:, :, :], in_=src[:, split:, :, :])
+                nc.scalar.copy(out=dst[:, c, split:, :, :], in_=src[:, c, split:, :, :])
             grouped_of[chunk] = grouped
 
         def quantise_weights(chunk):
@@ -176,8 +177,7 @@ def tile_matchingnet_pb_kernel(tc, p, q, W1, b1, W2, b2, out):
                                     words_of_table[e][:, first : first + P],
                                     ident_f32[:],
                                 )
-                        copy = nc.scalar.copy if pair % 2 == 0 else nc.vector.tensor_copy
-                        copy(
+                        nc.scalar.copy(
                             out=x_words[:, pair * 2 * P : (pair + 1) * 2 * P, :],
                             in_=bank[:].rearrange("r e n -> r n e"),
                         )
@@ -217,7 +217,7 @@ def tile_matchingnet_pb_kernel(tc, p, q, W1, b1, W2, b2, out):
                 in_=hidden_of[block][:].rearrange("r n t -> r (n t)"),
             )
 
-        def finish_output(block, first_tile):
+        def add_output_bias(block, first_tile):
             cols = slice(block * BLOCK_COLS, (block + 1) * BLOCK_COLS)
             biased = result_pool.tile([P, 2, BLOCK_COLS], F32, tag="biased_out")
             for s in range(2):
@@ -227,6 +227,11 @@ def tile_matchingnet_pb_kernel(tc, p, q, W1, b1, W2, b2, out):
                     in1=b2_all[:, cols],
                     op=ALU.add,
                 )
+            biased_out_of[block, first_tile] = biased
+
+        def leaky_output(block, first_tile):
+            cols = slice(block * BLOCK_COLS, (block + 1) * BLOCK_COLS)
+            biased = biased_out_of[block, first_tile]
             result = result_pool.tile([P, 2, BLOCK_COLS], F32)
             nc.vector.scalar_tensor_tensor(
                 out=result[:], in0=biased[:], scalar=SLOPE, in1=biased[:], op0=ALU.mult, op1=ALU.max
@@ -269,7 +274,9 @@ def tile_matchingnet_pb_kernel(tc, p, q, W1, b1, W2, b2, out):
                 add_hidden_bias(completed(step, BIAS_LAG, 0))
             if completed(step, LEAKY_LAG, 0) is not None:
                 leaky_hidden(completed(step, LEAKY_LAG, 0))
-            if completed(step, FINISH_LAG, 1) is not None:
-                finish_output(completed(step, FINISH_LAG, 1), 0)
-            if completed(step, FINISH_LAG + 1, 1) is not None:
-                finish_output(completed(step, FINISH_LAG + 1, 1), 2)
+            for half_lag, first_tile in ((0, 0), (1, 2)):
+                if completed(step, FINISH_LAG + half_lag, 1) is not None:
+                    add_output_bias(completed(step, FINISH_LAG + half_lag, 1), first_tile)
+            for half_lag, first_tile in ((0, 0), (1, 2)):
+                if completed(step, FINISH_LAG + half_lag + 1, 1) is not None:
+                    leaky_output(completed(step, FINISH_LAG + half_lag + 1, 1), first_tile)

from contextlib import ExitStack

import concourse.mybir as mybir
from concourse.masks import make_identity

F32 = mybir.dt.float32
BF16 = mybir.dt.bfloat16
U32 = mybir.dt.uint32
U8 = mybir.dt.uint8
FP8X4 = mybir.dt.float8_e4m3fn_x4
ALU = mybir.AluOpType
ACT = mybir.ActivationFunctionType

P = 128
PACK = 4
K_PASS = P * PACK
BATCH = 512
WIDTH = 2048
SLOPE = 0.01
PASSES = WIDTH // K_PASS
SAMPLE_TILES = BATCH // P

BLOCK_COLS = 512
BLOCKS = WIDTH // BLOCK_COLS
BLOCK_BANKS = 4
CHUNK_PASSES = 2
CHUNK_ROWS = CHUNK_PASSES * K_PASS
BLOCK_CHUNKS = PASSES // CHUNK_PASSES
LAYER_CHUNKS = BLOCKS * BLOCK_CHUNKS
CHUNKS = 2 * LAYER_CHUNKS

RAW_BUFS = 10
RUN = 4

VECTOR_COLS = 256
VECTOR_CHUNKS = 11

QUANTISE_LAG = 1
MULTIPLY_LAG = 2
BIAS_LAG = 2
LEAKY_LAG = 3
REQUANTISE_LAG = 4
FINISH_LAG = 2

FLOPS = 2 * 2 * BATCH * WIDTH * WIDTH


def tile_matchingnet_pb_kernel(tc, p, q, W1, b1, W2, b2, out):
    nc = tc.nc
    with ExitStack() as ctx:
        keep = ctx.enter_context(tc.tile_pool(name="keep", bufs=1))
        raw_pool = ctx.enter_context(tc.tile_pool(name="raw", bufs=RAW_BUFS))
        grouped_pool = ctx.enter_context(tc.tile_pool(name="grouped", bufs=4))
        weight_pool = ctx.enter_context(tc.tile_pool(name="weight", bufs=4))
        hidden_pool = ctx.enter_context(tc.tile_pool(name="hidden", bufs=2))
        result_pool = ctx.enter_context(tc.tile_pool(name="result", bufs=3))
        psum = ctx.enter_context(tc.psum_pool(name="psum", bufs=8))

        raw_of = {}
        grouped_of = {}
        codes_of = {}
        scales_of = {}
        banks_of = {}
        biased_of = {}
        hidden_of = {}
        biased_out_of = {}

        x_codes = keep.tile([P, PASSES, BATCH], U32, align_bytes=64)
        x_scales = keep.tile([P, PASSES, BATCH], U8, align_bytes=64)
        h_codes = keep.tile([P, PASSES, BATCH], U32, align_bytes=64)
        h_scales = keep.tile([P, PASSES, BATCH], U8, align_bytes=64)
        p_rows = keep.tile([P, SAMPLE_TILES * WIDTH // 2], BF16)
        q_rows = keep.tile([P, SAMPLE_TILES * WIDTH // 2], BF16)
        b1_rows = keep.tile([P, P], BF16)
        b1_cols = keep.tile([P, WIDTH // P], F32)
        b2_all = keep.tile([P, WIDTH], BF16)
        ident_f32 = keep.tile([P, P], F32)
        ident_bf16 = keep.tile([P, P], BF16)

        def place(chunk):
            layer, rest = divmod(chunk, LAYER_CHUNKS)
            block, half = divmod(rest, BLOCK_CHUNKS)
            return layer, block, half

        def load_weights(chunk):
            layer, block, half = place(chunk)
            rows = slice(half * CHUNK_ROWS, (half + 1) * CHUNK_ROWS)
            cols = slice(block * BLOCK_COLS, (block + 1) * BLOCK_COLS)
            raw = raw_pool.tile([P, CHUNK_PASSES, PACK, BLOCK_COLS], BF16)
            if layer == 0:
                by_table = W1[rows, cols].rearrange(
                    "(c r u e) w -> c e r u w", c=CHUNK_PASSES, u=2, e=2
                )
                for c in range(CHUNK_PASSES):
                    for e in range(2):
                        nc.sync.dma_start(out=raw[:, c, 2 * e : 2 * e + 2, :], in_=by_table[c, e])
            else:
                by_pass = W2[rows, cols].rearrange("(c t r) w -> c r t w", c=CHUNK_PASSES, r=P)
                for c in range(CHUNK_PASSES):
                    nc.sync.dma_start(out=raw[:, c, :, :], in_=by_pass[c])
            raw_of[chunk] = raw

        def regroup(chunk):
            split = (VECTOR_COLS if chunk < VECTOR_CHUNKS else 0) // RUN
            raw = raw_of[chunk]
            grouped = grouped_pool.tile([P, CHUNK_PASSES, BLOCK_COLS, PACK], BF16, align_bytes=64)
            src = raw[:].rearrange("r c t (w i) -> r c w t i", i=RUN)
            dst = grouped[:].rearrange("r c (w i) t -> r c w t i", i=RUN)
            if split > 0:
                nc.vector.tensor_copy(out=dst[:, :, :split, :, :], in_=src[:, :, :split, :, :])
            for c in range(CHUNK_PASSES):
                nc.scalar.copy(out=dst[:, c, split:, :, :], in_=src[:, c, split:, :, :])
            grouped_of[chunk] = grouped

        def quantise_weights(chunk):
            codes = weight_pool.tile([P, CHUNK_PASSES * BLOCK_COLS], U32, align_bytes=64)
            scales = weight_pool.tile([P, CHUNK_PASSES * BLOCK_COLS], U8, align_bytes=64)
            nc.vector.quantize_mx(
                out=codes[:].bitcast(FP8X4),
                scales=scales[:],
                in_=grouped_of[chunk][:].rearrange("r c w t -> r (c w t)"),
            )
            codes_of[chunk] = codes
            scales_of[chunk] = scales

        def multiply(chunk):
            layer, block, half = place(chunk)
            if half == 0:
                banks_of[layer, block] = [
                    psum.tile([P, BLOCK_COLS], F32, tag="bank", name="acc%d" % b)
                    for b in range(BLOCK_BANKS)
                ]
            codes = codes_of[chunk]
            scales = scales_of[chunk]
            for b in range(BLOCK_BANKS):
                tile_cols = slice(b * P, (b + 1) * P)
                for c in range(CHUNK_PASSES):
                    k_pass = half * CHUNK_PASSES + c
                    first = c * BLOCK_COLS
                    if layer == 0:
                        units = slice(first + b * P, first + (b + 1) * P)
                        lhsT, lhsT_scale = codes[:, units], scales[:, units]
                        rhs, rhs_scale = x_codes[:, k_pass, :], x_scales[:, k_pass, :]
                    else:
                        lhsT, lhsT_scale = h_codes[:, k_pass, tile_cols], h_scales[:, k_pass, tile_cols]
                        columns = slice(first, first + BLOCK_COLS)
                        rhs, rhs_scale = codes[:, columns], scales[:, columns]
                    nc.tensor.matmul_mx(
                        out=banks_of[layer, block][b][:],
                        lhsT=lhsT.bitcast(FP8X4),
                        lhsT_scale=lhsT_scale,
                        rhs=rhs.bitcast(FP8X4),
                        rhs_scale=rhs_scale,
                        start=(k_pass == 0),
                        stop=(k_pass == PASSES - 1),
                    )

        def prepare_inputs():
            b1_bank = psum.tile([P, P], BF16, tag="bank")
            nc.tensor.transpose(b1_bank[:], b1_rows[:], ident_bf16[:])
            nc.vector.tensor_copy(out=b1_cols[:], in_=b1_bank[:, : WIDTH // P])

            words_of_table = (p_rows[:].bitcast(F32), q_rows[:].bitcast(F32))
            sample_words = WIDTH // 4
            grouped_x = {}
            for k_pass in range(PASSES + 1):
                if k_pass < PASSES:
                    x_tile = hidden_pool.tile([P, BATCH * PACK], BF16, tag="x", align_bytes=64)
                    x_words = x_tile[:].bitcast(F32).rearrange("r (n e) -> r n e", e=2)
                    for pair in range(SAMPLE_TILES // 2):
                        bank = psum.tile([P, 2, 2 * P], F32, tag="bank")
                        for e in range(2):
                            for s in range(2):
                                first = (2 * pair + s) * sample_words + k_pass * P
                                nc.tensor.transpose(
                                    bank[:, e, s * P : (s + 1) * P],
                                    words_of_table[e][:, first : first + P],
                                    ident_f32[:],
                                )
                        nc.scalar.copy(
                            out=x_words[:, pair * 2 * P : (pair + 1) * 2 * P, :],
                            in_=bank[:].rearrange("r e n -> r n e"),
                        )
                    grouped_x[k_pass] = x_tile
                if k_pass > 0:
                    nc.vector.quantize_mx(
                        out=x_codes[:, k_pass - 1, :].bitcast(FP8X4),
                        scales=x_scales[:, k_pass - 1, :],
                        in_=grouped_x[k_pass - 1][:],
                    )

        def add_hidden_bias(block):
            biased = hidden_pool.tile([P, PACK, BATCH], F32)
            for t in range(PACK):
                unit_tile = block * PACK + t
                nc.scalar.activation(
                    out=biased[:, t, :],
                    in_=banks_of[0, block][t][:],
                    func=ACT.Identity,
                    bias=b1_cols[:, unit_tile : unit_tile + 1],
                    scale=1.0,
                )
            biased_of[block] = biased

        def leaky_hidden(block):
            hidden = hidden_pool.tile([P, BATCH, PACK], BF16, align_bytes=64)
            by_sample = biased_of[block][:].rearrange("r t n -> r n t")
            nc.vector.scalar_tensor_tensor(
                out=hidden[:], in0=by_sample, scalar=SLOPE, in1=by_sample, op0=ALU.mult, op1=ALU.max
            )
            hidden_of[block] = hidden

        def quantise_hidden(block):
            nc.vector.quantize_mx(
                out=h_codes[:, block, :].bitcast(FP8X4),
                scales=h_scales[:, block, :],
                in_=hidden_of[block][:].rearrange("r n t -> r (n t)"),
            )

        def add_output_bias(block, first_tile):
            cols = slice(block * BLOCK_COLS, (block + 1) * BLOCK_COLS)
            biased = result_pool.tile([P, 2, BLOCK_COLS], F32, tag="biased_out")
            for s in range(2):
                nc.vector.tensor_tensor(
                    out=biased[:, s, :],
                    in0=banks_of[1, block][first_tile + s][:],
                    in1=b2_all[:, cols],
                    op=ALU.add,
                )
            biased_out_of[block, first_tile] = biased

        def leaky_output(block, first_tile):
            cols = slice(block * BLOCK_COLS, (block + 1) * BLOCK_COLS)
            biased = biased_out_of[block, first_tile]
            result = result_pool.tile([P, 2, BLOCK_COLS], F32)
            nc.vector.scalar_tensor_tensor(
                out=result[:], in0=biased[:], scalar=SLOPE, in1=biased[:], op0=ALU.mult, op1=ALU.max
            )
            rows = out.rearrange("(r s) j -> r s j", s=SAMPLE_TILES)
            nc.sync.dma_start(out=rows[:, first_tile : first_tile + 2, cols], in_=result[:])

        make_identity(nc, ident_f32[:])
        make_identity(nc, ident_bf16[:])
        nc.vector.memset(b1_rows[:], 0.0)
        nc.scalar.dma_start(out=b1_rows[: WIDTH // P, :], in_=b1.rearrange("(t r) -> t r", r=P))
        load_weights(0)
        nc.sync.dma_start(out=p_rows[:], in_=p.rearrange("(r s) i j -> r (s i j)", s=SAMPLE_TILES))
        nc.sync.dma_start(out=q_rows[:], in_=q.rearrange("(r s) i j -> r (s i j)", s=SAMPLE_TILES))
        for chunk in range(1, RAW_BUFS):
            load_weights(chunk)
        nc.sync.dma_start(out=b2_all[:], in_=b2.partition_broadcast(P))

        def completed(step, lag, layer):
            chunk = step - lag
            if 0 <= chunk < CHUNKS and chunk % BLOCK_CHUNKS == BLOCK_CHUNKS - 1:
                if place(chunk)[0] == layer:
                    return place(chunk)[1]
            return None

        for step in range(CHUNKS + FINISH_LAG + 2):
            if step < CHUNKS:
                regroup(step)
            if step + RAW_BUFS < CHUNKS:
                load_weights(step + RAW_BUFS)
            if step == 0:
                prepare_inputs()
            if completed(step, REQUANTISE_LAG, 0) is not None:
                quantise_hidden(completed(step, REQUANTISE_LAG, 0))
            if 0 <= step - QUANTISE_LAG < CHUNKS:
                quantise_weights(step - QUANTISE_LAG)
            if 0 <= step - MULTIPLY_LAG < CHUNKS:
                multiply(step - MULTIPLY_LAG)
            if completed(step, BIAS_LAG, 0) is not None:
                add_hidden_bias(completed(step, BIAS_LAG, 0))
            if completed(step, LEAKY_LAG, 0) is not None:
                leaky_hidden(completed(step, LEAKY_LAG, 0))
            for half_lag, first_tile in ((0, 0), (1, 2)):
                if completed(step, FINISH_LAG + half_lag, 1) is not None:
                    add_output_bias(completed(step, FINISH_LAG + half_lag, 1), first_tile)
            for half_lag, first_tile in ((0, 0), (1, 2)):
                if completed(step, FINISH_LAG + half_lag + 1, 1) is not None:
                    leaky_output(completed(step, FINISH_LAG + half_lag + 1, 1), first_tile)
